import numpy as np
import ml_dtypes


def mxq(x, axis, fmt="e4m3"):
    dtype, down = {"e4m3": (ml_dtypes.float8_e4m3fn, 7), "e5m2": (ml_dtypes.float8_e5m2, 14)}[fmt]
    v = np.moveaxis(np.asarray(x, np.float32).astype(ml_dtypes.bfloat16).astype(np.float64), axis, -1)
    blocks = v.reshape(v.shape[:-1] + (-1, 32))
    amax = np.abs(blocks).max(-1, keepdims=True)
    byte = np.maximum(np.where(amax > 0, np.frexp(amax)[1] - 1 + 127, 0) - down, 1)
    scale = np.exp2(byte - 127.0)
    codes = (blocks / scale).astype(np.float32).astype(dtype).astype(np.float64)
    return np.moveaxis((codes * scale).reshape(v.shape), -1, axis)


WIDE = False


def mx_kscale(k):
    if not WIDE:
        return np.ones(k)
    levels = np.array([10, -10, 5, -5, 0])
    a = np.random.permutation(np.resize(levels, k // 512 * 4)).reshape(k // 512, 4)
    idx = np.arange(k)
    return np.exp2(a[idx // 512, idx % 128 // 32])


BF16 = ml_dtypes.bfloat16


def bf(x):
    return np.asarray(x, np.float32).astype(BF16)


def f64(x):
    return np.asarray(x).astype(np.float64)


B, C, HH, WW, NH = 4, 512, 16, 16, 8
N = HH * WW
DH = C // NH
HALF = C // 2


def pos_encoding():
    positions = np.arange(N, dtype=np.float64)
    depths = np.arange(HALF, dtype=np.float64) / HALF
    angle_rates = 1.0 / (10000.0 ** depths)
    angle_rads = positions[:, None] * angle_rates[None, :]
    return np.concatenate([np.sin(angle_rads), np.cos(angle_rads)], axis=-1)


def heads(t):
    return t.reshape(B, N, NH, DH).transpose(0, 2, 1, 3)


def setup_inputs():
    bound = np.sqrt(6.0 / (C + 3 * C))
    s = mx_kscale(C)
    u = s / s.min()
    return {"x": bf(np.random.standard_normal((B, C, HH, WW)) * u[None, :, None, None]),
            "W_qkv": bf(np.random.uniform(-bound, bound, (3 * C, C)) / u[None, :])}


def reference(x, W_qkv):
    xt = f64(x).reshape(B, C, N) + pos_encoding().T[None]
    tokens = xt.transpose(0, 2, 1)
    qkv = mxq(tokens, 2, "e4m3") @ mxq(f64(W_qkv), 1, "e4m3").T
    q, k, v = np.split(qkv, 3, axis=-1)
    return heads(q), heads(k), heads(v)

@@ -1,0 +1,220 @@
+import math
+from contextlib import ExitStack
+
+import concourse.mybir as mybir
+from concourse.masks import make_identity
+
+F32 = mybir.dt.float32
+BF16 = mybir.dt.bfloat16
+I32 = mybir.dt.int32
+U32 = mybir.dt.uint32
+U8 = mybir.dt.uint8
+FP8X4 = mybir.dt.float8_e4m3fn_x4
+ALU = mybir.AluOpType
+ACT = mybir.ActivationFunctionType
+
+P = 128
+PACK = 4
+IMAGES = 4
+CHANNELS = 512
+POSITIONS = 256
+HEADS = 8
+HEAD_DIM = 64
+PROJECTIONS = 3
+PROJ_COLS = HEADS * HEAD_DIM
+W_BLOCKS = PROJ_COLS // P
+
+PAIR = 2
+RUN = 4
+ROWS = POSITIONS // RUN
+TABLE_CHUNKS = 2
+
+RATES = CHANNELS // 2
+ROUND = 1.5 * 2.0**23
+
+FLOPS = 2 * IMAGES * POSITIONS * CHANNELS * PROJECTIONS * PROJ_COLS
+
+
+def tile_multiheadselfattention_pa_kernel(tc, x, W_qkv, out_0, out_1, out_2):
+    nc = tc.nc
+    outs = (out_0, out_1, out_2)
+    with ExitStack() as pools:
+        keep = pools.enter_context(tc.tile_pool(name="keep", bufs=1))
+        stage_pool = pools.enter_context(tc.tile_pool(name="stage", bufs=6))
+        psum_w = pools.enter_context(tc.psum_pool(name="psum_w", bufs=4))
+        psum_acc = pools.enter_context(tc.psum_pool(name="psum_acc", bufs=4))
+        pools.enter_context(tc.manual_schedule())
+
+        x_rows = keep.tile([P, IMAGES * PACK, POSITIONS], BF16)
+        w_rows = keep.tile([P, PROJECTIONS, W_BLOCKS, CHANNELS], BF16)
+
+        def load_x(pair):
+            nc.sync.dma_start(
+                out=x_rows[:, pair * PAIR * PACK : (pair + 1) * PAIR * PACK, :].rearrange(
+                    "q (b u e) n -> q b u (e n)", b=PAIR, u=2
+                ),
+                in_=x[pair * PAIR : (pair + 1) * PAIR].rearrange(
+                    "b (u q e) h w -> q b u (e h w)", u=2, e=2
+                ),
+            )
+
+        def load_w(s):
+            nc.sync.dma_start(
+                out=w_rows[:, s],
+                in_=W_qkv[s * PROJ_COLS : (s + 1) * PROJ_COLS, :].rearrange(
+                    "(g o) c -> o g c", o=P
+                ),
+            )
+
+        load_w(0)
+        load_x(0)
+        load_w(1)
+        load_w(2)
+        load_x(1)
+
+        chan_int = keep.tile([P, 2], I32)
+        nc.gpsimd.iota(chan_int[:], pattern=[[1, 2]], base=0, channel_multiplier=2)
+        base = keep.tile([P, 2], F32)
+        nc.gpsimd.memset(base[:], 10000.0)
+        pos_int = keep.tile([P, POSITIONS], I32)
+        nc.gpsimd.iota(pos_int[:], pattern=[[1, POSITIONS]], base=0, channel_multiplier=0)
+        exponent = keep.tile([P, 2], F32)
+        nc.vector.tensor_scalar_mul(out=exponent[:], in0=chan_int[:], scalar1=-1.0 / RATES)
+        rate = keep.tile([P, 2], F32)
+        nc.gpsimd.tensor_tensor(out=rate[:], in0=base[:], in1=exponent[:], op=ALU.pow)
+        pos = keep.tile([P, POSITIONS], F32)
+        nc.vector.tensor_scalar_mul(out=pos[:], in0=pos_int[:], scalar1=1.0 / (2.0 * math.pi))
+
+        ident = keep.tile([P, P], F32)
+        make_identity(nc, ident[:])
+        warm = keep.tile([P, 2], F32)
+        nc.vector.memset(warm[:, 0:1], 0.0)
+        nc.scalar.activation(out=warm[:, 1:2], in_=warm[:, 0:1], func=ACT.Sin)
+
+        w_codes = keep.tile([P, PROJECTIONS, PROJ_COLS], U32, align_bytes=64)
+        w_scales = keep.tile([P, PROJECTIONS, PROJ_COLS], U8, align_bytes=64)
+        w_grouped = keep.tile([P, PROJECTIONS, PROJ_COLS, PACK], BF16, align_bytes=64)
+
+        def transpose_w(s):
+            words = w_rows[:, s].bitcast(F32)
+            grouped_words = w_grouped[:, s].bitcast(F32)
+            for half in range(2):
+                flipped = psum_w.tile([P, 2, 2, P], F32)
+                for g in range(2):
+                    for u in range(2):
+                        nc.tensor.transpose(
+                            flipped[:, g, u, :],
+                            words[:, 2 * half + g, u * P : (u + 1) * P],
+                            ident[:],
+                        )
+                nc.scalar.copy(
+                    out=grouped_words[:, half * 2 * P : (half + 1) * 2 * P, :].rearrange(
+                        "q (g o) u -> q g o u", g=2
+                    ),
+                    in_=flipped[:].rearrange("q g u o -> q g o u"),
+                )
+
+        def quantise_w(s):
+            nc.vector.quantize_mx(
+                out=w_codes[:, s, :].bitcast(FP8X4),
+                scales=w_scales[:, s, :],
+                in_=w_grouped[:, s].rearrange("q c t -> q (c t)"),
+            )
+
+        transpose_w(0)
+
+        turns = keep.tile([P, PACK, POSITIONS], F32)
+        for u in range(2):
+            for e in range(2):
+                nc.vector.tensor_scalar(
+                    out=turns[:, 2 * u + e, :],
+                    in0=pos[:],
+                    scalar1=rate[:, e : e + 1],
+                    scalar2=0.25 * u,
+                    op0=ALU.mult,
+                    op1=ALU.add,
+                )
+        whole = keep.tile([P, PACK, POSITIONS], F32)
+        frac = keep.tile([P, PACK, POSITIONS], F32)
+        pe = keep.tile([P, PAIR * PACK, POSITIONS], F32)
+        chunk_positions = POSITIONS // TABLE_CHUNKS
+        for chunk in range(TABLE_CHUNKS):
+            span = slice(chunk * chunk_positions, (chunk + 1) * chunk_positions)
+            nc.vector.tensor_scalar(
+                out=whole[:, :, span],
+                in0=turns[:, :, span],
+                scalar1=ROUND,
+                scalar2=ROUND,
+                op0=ALU.add,
+                op1=ALU.subtract,
+            )
+            nc.vector.tensor_tensor(
+                out=frac[:, :, span], in0=turns[:, :, span], in1=whole[:, :, span], op=ALU.subtract
+            )
+            nc.scalar.activation(
+                out=pe[:, :, span].rearrange("q (b t) n -> q b t n", b=PAIR),
+                in_=frac[:, :, span].unsqueeze(1).to_broadcast([P, PAIR, PACK, chunk_positions]),
+                func=ACT.Sin,
+                scale=2.0 * math.pi,
+            )
+
+        quantise_w(0)
+        transpose_w(1)
+        transpose_w(2)
+
+        tok = keep.tile([P, IMAGES // PAIR, RUN, ROWS, PAIR * PACK], BF16, align_bytes=64)
+        tok_codes = keep.tile([P, IMAGES // PAIR, RUN * P], U32, align_bytes=64)
+        tok_scales = keep.tile([P, IMAGES // PAIR, RUN * P], U8, align_bytes=64)
+
+        def quantise_tokens(pair):
+            chunk_rows = ROWS // TABLE_CHUNKS
+            for chunk in range(TABLE_CHUNKS):
+                span = slice(chunk * chunk_positions, (chunk + 1) * chunk_positions)
+                rows = slice(chunk * chunk_rows, (chunk + 1) * chunk_rows)
+                nc.vector.tensor_tensor(
+                    out=tok[:, pair, :, rows, :].rearrange("q r i g -> q i g r"),
+                    in0=x_rows[:, pair * PAIR * PACK : (pair + 1) * PAIR * PACK, span].rearrange(
+                        "q g (i r) -> q i g r", r=RUN
+                    ),
+                    in1=pe[:, :, span].rearrange("q g (i r) -> q i g r", r=RUN),
+                    op=ALU.add,
+                )
+            nc.vector.quantize_mx(
+                out=tok_codes[:, pair, :].bitcast(FP8X4),
+                scales=tok_scales[:, pair, :],
+                in_=tok[:, pair].rearrange("q r i g -> q (r i g)"),
+            )
+
+        def project(pair, s, vector_helps):
+            stage = stage_pool.tile([P, HEADS, RUN, HEAD_DIM], F32)
+            for r in range(RUN):
+                acc = psum_acc.tile([P, PROJ_COLS], F32)
+                nc.tensor.matmul_mx(
+                    out=acc[:],
+                    lhsT=tok_codes[:, pair, r * P : (r + 1) * P].bitcast(FP8X4),
+                    lhsT_scale=tok_scales[:, pair, r * P : (r + 1) * P],
+                    rhs=w_codes[:, s, :].bitcast(FP8X4),
+                    rhs_scale=w_scales[:, s, :],
+                    start=True,
+                    stop=True,
+                )
+                by_head = acc[:].rearrange("m (h d) -> m h d", d=HEAD_DIM)
+                if vector_helps and r % 2 == 1:
+                    nc.vector.tensor_copy(out=stage[:, :, r, :], in_=by_head)
+                else:
+                    nc.scalar.copy(out=stage[:, :, r, :], in_=by_head)
+            for b in range(PAIR):
+                nc.sync.dma_start(
+                    out=outs[s][pair * PAIR + b].rearrange("h (i r) d -> i h (r d)", r=RUN),
+                    in_=stage[b:P:PAIR].rearrange("m h r d -> m h (r d)"),
+                )
+
+        quantise_tokens(0)
+        quantise_w(1)
+        project(0, 0, True)
+        quantise_w(2)
+        quantise_tokens(1)
+        project(0, 1, False)
+        project(0, 2, False)
+        for s in range(PROJECTIONS):
+            project(1, s, True)

@@ -27,7 +27,7 @@ W_BLOCKS = PROJ_COLS // P
 PAIR = 2
 RUN = 4
 ROWS = POSITIONS // RUN
-TABLE_CHUNKS = 2
+TABLE_CHUNKS = 4
 
 RATES = CHANNELS // 2
 ROUND = 1.5 * 2.0**23
@@ -66,8 +66,8 @@ def tile_multiheadselfattention_pa_kernel(tc, x, W_qkv, out_0, out_1, out_2):
                 ),
             )
 
-        load_w(0)
         load_x(0)
+        load_w(0)
         load_w(1)
         load_w(2)
         load_x(1)
@@ -90,6 +90,8 @@ def tile_multiheadselfattention_pa_kernel(tc, x, W_qkv, out_0, out_1, out_2):
         warm = keep.tile([P, 2], F32)
         nc.vector.memset(warm[:, 0:1], 0.0)
         nc.scalar.activation(out=warm[:, 1:2], in_=warm[:, 0:1], func=ACT.Sin)
+        quarter_turn = keep.tile([P, 1], F32)
+        nc.vector.tensor_scalar_add(out=quarter_turn[:], in0=warm[:, 0:1], scalar1=0.5 * math.pi)
 
         w_codes = keep.tile([P, PROJECTIONS, PROJ_COLS], U32, align_bytes=64)
         w_scales = keep.tile([P, PROJECTIONS, PROJ_COLS], U8, align_bytes=64)
@@ -97,7 +99,7 @@ def tile_multiheadselfattention_pa_kernel(tc, x, W_qkv, out_0, out_1, out_2):
 
         def transpose_w(s):
             words = w_rows[:, s].bitcast(F32)
-            grouped_words = w_grouped[:, s].bitcast(F32)
+            halves = []
             for half in range(2):
                 flipped = psum_w.tile([P, 2, 2, P], F32)
                 for g in range(2):
@@ -107,11 +109,17 @@ def tile_multiheadselfattention_pa_kernel(tc, x, W_qkv, out_0, out_1, out_2):
                             words[:, 2 * half + g, u * P : (u + 1) * P],
                             ident[:],
                         )
+                halves.append(flipped)
+            return halves
+
+        def group_w(s, halves):
+            grouped_words = w_grouped[:, s].bitcast(F32)
+            for half in range(2):
                 nc.scalar.copy(
                     out=grouped_words[:, half * 2 * P : (half + 1) * 2 * P, :].rearrange(
                         "q (g o) u -> q g o u", g=2
                     ),
-                    in_=flipped[:].rearrange("q g u o -> q g o u"),
+                    in_=halves[half][:].rearrange("q g u o -> q g o u"),
                 )
 
         def quantise_w(s):
@@ -121,25 +129,18 @@ def tile_multiheadselfattention_pa_kernel(tc, x, W_qkv, out_0, out_1, out_2):
                 in_=w_grouped[:, s].rearrange("q c t -> q (c t)"),
             )
 
-        transpose_w(0)
-
-        turns = keep.tile([P, PACK, POSITIONS], F32)
-        for u in range(2):
-            for e in range(2):
-                nc.vector.tensor_scalar(
-                    out=turns[:, 2 * u + e, :],
-                    in0=pos[:],
-                    scalar1=rate[:, e : e + 1],
-                    scalar2=0.25 * u,
-                    op0=ALU.mult,
-                    op1=ALU.add,
-                )
-        whole = keep.tile([P, PACK, POSITIONS], F32)
-        frac = keep.tile([P, PACK, POSITIONS], F32)
+        turns = keep.tile([P, 2, POSITIONS], F32)
+        for e in range(2):
+            nc.vector.tensor_scalar_mul(out=turns[:, e, :], in0=pos[:], scalar1=rate[:, e : e + 1])
+        whole = keep.tile([P, 2, POSITIONS], F32)
+        frac = keep.tile([P, 2, POSITIONS], F32)
+        size = keep.tile([P, 2, POSITIONS], F32)
         pe = keep.tile([P, PAIR * PACK, POSITIONS], F32)
+        pe_parts = pe[:].rearrange("q (b u e) n -> q b u e n", b=PAIR, u=2)
         chunk_positions = POSITIONS // TABLE_CHUNKS
         for chunk in range(TABLE_CHUNKS):
             span = slice(chunk * chunk_positions, (chunk + 1) * chunk_positions)
+            both = [P, PAIR, 2, chunk_positions]
             nc.vector.tensor_scalar(
                 out=whole[:, :, span],
                 in0=turns[:, :, span],
@@ -152,21 +153,38 @@ def tile_multiheadselfattention_pa_kernel(tc, x, W_qkv, out_0, out_1, out_2):
                 out=frac[:, :, span], in0=turns[:, :, span], in1=whole[:, :, span], op=ALU.subtract
             )
             nc.scalar.activation(
-                out=pe[:, :, span].rearrange("q (b t) n -> q b t n", b=PAIR),
-                in_=frac[:, :, span].unsqueeze(1).to_broadcast([P, PAIR, PACK, chunk_positions]),
+                out=pe_parts[:, :, 0, :, span],
+                in_=frac[:, :, span].unsqueeze(1).to_broadcast(both),
                 func=ACT.Sin,
                 scale=2.0 * math.pi,
             )
+            nc.vector.scalar_tensor_tensor(
+                out=size[:, :, span],
+                in0=frac[:, :, span],
+                scalar=-1.0,
+                in1=frac[:, :, span],
+                op0=ALU.mult,
+                op1=ALU.max,
+            )
+            nc.scalar.activation(
+                out=pe_parts[:, :, 1, :, span],
+                in_=size[:, :, span].unsqueeze(1).to_broadcast(both),
+                func=ACT.Sin,
+                scale=-2.0 * math.pi,
+                bias=quarter_turn[:],
+            )
 
-        quantise_w(0)
-        transpose_w(1)
-        transpose_w(2)
+        flipped_q = transpose_w(0)
+        flipped_k = transpose_w(1)
+        group_w(0, flipped_q)
+        flipped_v = transpose_w(2)
+        group_w(1, flipped_k)
 
         tok = keep.tile([P, IMAGES // PAIR, RUN, ROWS, PAIR * PACK], BF16, align_bytes=64)
         tok_codes = keep.tile([P, IMAGES // PAIR, RUN * P], U32, align_bytes=64)
         tok_scales = keep.tile([P, IMAGES // PAIR, RUN * P], U8, align_bytes=64)
 
-        def quantise_tokens(pair):
+        def add_table(pair):
             chunk_rows = ROWS // TABLE_CHUNKS
             for chunk in range(TABLE_CHUNKS):
                 span = slice(chunk * chunk_positions, (chunk + 1) * chunk_positions)
@@ -179,11 +197,14 @@ def tile_multiheadselfattention_pa_kernel(tc, x, W_qkv, out_0, out_1, out_2):
                     in1=pe[:, :, span].rearrange("q g (i r) -> q i g r", r=RUN),
                     op=ALU.add,
                 )
-            nc.vector.quantize_mx(
-                out=tok_codes[:, pair, :].bitcast(FP8X4),
-                scales=tok_scales[:, pair, :],
-                in_=tok[:, pair].rearrange("q r i g -> q (r i g)"),
-            )
+
+        def quantise_tokens(pair):
+            for r in range(RUN):
+                nc.vector.quantize_mx(
+                    out=tok_codes[:, pair, r * P : (r + 1) * P].bitcast(FP8X4),
+                    scales=tok_scales[:, pair, r * P : (r + 1) * P],
+                    in_=tok[:, pair, r].rearrange("q i g -> q (i g)"),
+                )
 
         def project(pair, s, vector_helps):
             stage = stage_pool.tile([P, HEADS, RUN, HEAD_DIM], F32)
@@ -209,10 +230,14 @@ def tile_multiheadselfattention_pa_kernel(tc, x, W_qkv, out_0, out_1, out_2):
                     in_=stage[b:P:PAIR].rearrange("m h r d -> m h (r d)"),
                 )
 
+        add_table(0)
+        quantise_w(0)
         quantise_tokens(0)
-        quantise_w(1)
         project(0, 0, True)
+        group_w(2, flipped_v)
+        quantise_w(1)
         quantise_w(2)
+        add_table(1)
         quantise_tokens(1)
         project(0, 1, False)
         project(0, 2, False)

@@ -18,21 +18,27 @@ PACK = 4
 IMAGES = 4
 CHANNELS = 512
 POSITIONS = 256
-HEADS = 8
 HEAD_DIM = 64
-PROJECTIONS = 3
-PROJ_COLS = HEADS * HEAD_DIM
-W_BLOCKS = PROJ_COLS // P
+BANK = 512
 
 PAIR = 2
+PAIRS = IMAGES // PAIR
 RUN = 4
 ROWS = POSITIONS // RUN
 TABLE_CHUNKS = 4
 
+UNIT_HEADS = 4
+UNIT_COLS = UNIT_HEADS * HEAD_DIM
+UNIT_BLOCKS = UNIT_COLS // P
+UNITS = 6
+UNITS_PER_OUTPUT = 2
+COPY_AHEAD = 4
+QUANTISE_AHEAD = 2
+
 RATES = CHANNELS // 2
 ROUND = 1.5 * 2.0**23
 
-FLOPS = 2 * IMAGES * POSITIONS * CHANNELS * PROJECTIONS * PROJ_COLS
+FLOPS = 2 * IMAGES * POSITIONS * CHANNELS * UNITS * UNIT_COLS
 
 
 def tile_multiheadselfattention_pa_kernel(tc, x, W_qkv, out_0, out_1, out_2):
@@ -41,12 +47,11 @@ def tile_multiheadselfattention_pa_kernel(tc, x, W_qkv, out_0, out_1, out_2):
     with ExitStack() as pools:
         keep = pools.enter_context(tc.tile_pool(name="keep", bufs=1))
         stage_pool = pools.enter_context(tc.tile_pool(name="stage", bufs=6))
-        psum_w = pools.enter_context(tc.psum_pool(name="psum_w", bufs=4))
-        psum_acc = pools.enter_context(tc.psum_pool(name="psum_acc", bufs=4))
+        psum = pools.enter_context(tc.psum_pool(name="psum", bufs=8))
         pools.enter_context(tc.manual_schedule())
 
         x_rows = keep.tile([P, IMAGES * PACK, POSITIONS], BF16)
-        w_rows = keep.tile([P, PROJECTIONS, W_BLOCKS, CHANNELS], BF16)
+        w_rows = keep.tile([P, UNITS, UNIT_BLOCKS, CHANNELS], BF16)
 
         def load_x(pair):
             nc.sync.dma_start(
@@ -58,113 +63,66 @@ def tile_multiheadselfattention_pa_kernel(tc, x, W_qkv, out_0, out_1, out_2):
                 ),
             )
 
-        def load_w(s):
+        load_x(0)
+        for unit in range(UNITS):
             nc.sync.dma_start(
-                out=w_rows[:, s],
-                in_=W_qkv[s * PROJ_COLS : (s + 1) * PROJ_COLS, :].rearrange(
+                out=w_rows[:, unit],
+                in_=W_qkv[unit * UNIT_COLS : (unit + 1) * UNIT_COLS, :].rearrange(
                     "(g o) c -> o g c", o=P
                 ),
             )
-
-        load_x(0)
-        load_w(0)
-        load_w(1)
-        load_w(2)
         load_x(1)
 
         chan_int = keep.tile([P, 2], I32)
         nc.gpsimd.iota(chan_int[:], pattern=[[1, 2]], base=0, channel_multiplier=2)
         base = keep.tile([P, 2], F32)
         nc.gpsimd.memset(base[:], 10000.0)
-        pos_int = keep.tile([P, POSITIONS], I32)
-        nc.gpsimd.iota(pos_int[:], pattern=[[1, POSITIONS]], base=0, channel_multiplier=0)
         exponent = keep.tile([P, 2], F32)
         nc.vector.tensor_scalar_mul(out=exponent[:], in0=chan_int[:], scalar1=-1.0 / RATES)
         rate = keep.tile([P, 2], F32)
         nc.gpsimd.tensor_tensor(out=rate[:], in0=base[:], in1=exponent[:], op=ALU.pow)
-        pos = keep.tile([P, POSITIONS], F32)
-        nc.vector.tensor_scalar_mul(out=pos[:], in0=pos_int[:], scalar1=1.0 / (2.0 * math.pi))
-
         ident = keep.tile([P, P], F32)
         make_identity(nc, ident[:])
+
         warm = keep.tile([P, 2], F32)
         nc.vector.memset(warm[:, 0:1], 0.0)
         nc.scalar.activation(out=warm[:, 1:2], in_=warm[:, 0:1], func=ACT.Sin)
         quarter_turn = keep.tile([P, 1], F32)
         nc.vector.tensor_scalar_add(out=quarter_turn[:], in0=warm[:, 0:1], scalar1=0.5 * math.pi)
 
-        w_codes = keep.tile([P, PROJECTIONS, PROJ_COLS], U32, align_bytes=64)
-        w_scales = keep.tile([P, PROJECTIONS, PROJ_COLS], U8, align_bytes=64)
-        w_grouped = keep.tile([P, PROJECTIONS, PROJ_COLS, PACK], BF16, align_bytes=64)
-
-        def transpose_w(s):
-            words = w_rows[:, s].bitcast(F32)
-            halves = []
-            for half in range(2):
-                flipped = psum_w.tile([P, 2, 2, P], F32)
-                for g in range(2):
-                    for u in range(2):
-                        nc.tensor.transpose(
-                            flipped[:, g, u, :],
-                            words[:, 2 * half + g, u * P : (u + 1) * P],
-                            ident[:],
-                        )
-                halves.append(flipped)
-            return halves
-
-        def group_w(s, halves):
-            grouped_words = w_grouped[:, s].bitcast(F32)
-            for half in range(2):
-                nc.scalar.copy(
-                    out=grouped_words[:, half * 2 * P : (half + 1) * 2 * P, :].rearrange(
-                        "q (g o) u -> q g o u", g=2
-                    ),
-                    in_=halves[half][:].rearrange("q g u o -> q g o u"),
-                )
-
-        def quantise_w(s):
-            nc.vector.quantize_mx(
-                out=w_codes[:, s, :].bitcast(FP8X4),
-                scales=w_scales[:, s, :],
-                in_=w_grouped[:, s].rearrange("q c t -> q (c t)"),
-            )
+        ones = keep.tile([P, POSITIONS], F32)
+        nc.vector.memset(ones[:], 1.0)
+        count = keep.tile([P, POSITIONS], F32)
+        nc.vector.tensor_tensor_scan(
+            out=count[:], data0=ones[:], data1=ones[:], initial=-1.0, op0=ALU.mult, op1=ALU.add
+        )
+        pos = keep.tile([P, POSITIONS], F32)
+        nc.vector.tensor_scalar_mul(out=pos[:], in0=count[:], scalar1=1.0 / (2.0 * math.pi))
 
         turns = keep.tile([P, 2, POSITIONS], F32)
         for e in range(2):
             nc.vector.tensor_scalar_mul(out=turns[:, e, :], in0=pos[:], scalar1=rate[:, e : e + 1])
         whole = keep.tile([P, 2, POSITIONS], F32)
+        nc.vector.tensor_scalar(
+            out=whole[:], in0=turns[:], scalar1=ROUND, scalar2=ROUND, op0=ALU.add, op1=ALU.subtract
+        )
         frac = keep.tile([P, 2, POSITIONS], F32)
+        nc.vector.tensor_tensor(out=frac[:], in0=turns[:], in1=whole[:], op=ALU.subtract)
         size = keep.tile([P, 2, POSITIONS], F32)
+        nc.vector.scalar_tensor_tensor(
+            out=size[:], in0=frac[:], scalar=-1.0, in1=frac[:], op0=ALU.mult, op1=ALU.max
+        )
         pe = keep.tile([P, PAIR * PACK, POSITIONS], F32)
         pe_parts = pe[:].rearrange("q (b u e) n -> q b u e n", b=PAIR, u=2)
         chunk_positions = POSITIONS // TABLE_CHUNKS
         for chunk in range(TABLE_CHUNKS):
             span = slice(chunk * chunk_positions, (chunk + 1) * chunk_positions)
             both = [P, PAIR, 2, chunk_positions]
-            nc.vector.tensor_scalar(
-                out=whole[:, :, span],
-                in0=turns[:, :, span],
-                scalar1=ROUND,
-                scalar2=ROUND,
-                op0=ALU.add,
-                op1=ALU.subtract,
-            )
-            nc.vector.tensor_tensor(
-                out=frac[:, :, span], in0=turns[:, :, span], in1=whole[:, :, span], op=ALU.subtract
-            )
             nc.scalar.activation(
                 out=pe_parts[:, :, 0, :, span],
                 in_=frac[:, :, span].unsqueeze(1).to_broadcast(both),
                 func=ACT.Sin,
                 scale=2.0 * math.pi,
-            )
-            nc.vector.scalar_tensor_tensor(
-                out=size[:, :, span],
-                in0=frac[:, :, span],
-                scalar=-1.0,
-                in1=frac[:, :, span],
-                op0=ALU.mult,
-                op1=ALU.max,
             )
             nc.scalar.activation(
                 out=pe_parts[:, :, 1, :, span],
@@ -174,29 +132,49 @@ def tile_multiheadselfattention_pa_kernel(tc, x, W_qkv, out_0, out_1, out_2):
                 bias=quarter_turn[:],
             )
 
-        flipped_q = transpose_w(0)
-        flipped_k = transpose_w(1)
-        group_w(0, flipped_q)
-        flipped_v = transpose_w(2)
-        group_w(1, flipped_k)
+        w_grouped = keep.tile([P, UNITS, UNIT_COLS, PACK], BF16, align_bytes=64)
+        w_codes = keep.tile([P, UNITS, UNIT_COLS], U32, align_bytes=64)
+        w_scales = keep.tile([P, UNITS, UNIT_COLS], U8, align_bytes=64)
 
-        tok = keep.tile([P, IMAGES // PAIR, RUN, ROWS, PAIR * PACK], BF16, align_bytes=64)
-        tok_codes = keep.tile([P, IMAGES // PAIR, RUN * P], U32, align_bytes=64)
-        tok_scales = keep.tile([P, IMAGES // PAIR, RUN * P], U8, align_bytes=64)
+        def transpose_w(unit):
+            words = w_rows[:, unit].bitcast(F32)
+            flipped = psum.tile([P, UNIT_BLOCKS, 2, P], F32, tag="bank")
+            for g in range(UNIT_BLOCKS):
+                for u in range(2):
+                    nc.tensor.transpose(
+                        flipped[:, g, u, :], words[:, g, u * P : (u + 1) * P], ident[:]
+                    )
+            return flipped
 
-        def add_table(pair):
+        def group_w(unit):
+            nc.scalar.copy(
+                out=w_grouped[:, unit].bitcast(F32).rearrange("q (g o) u -> q g o u", g=UNIT_BLOCKS),
+                in_=flipped_w[unit][:].rearrange("q g u o -> q g o u"),
+            )
+
+        def quantise_w(unit):
+            nc.vector.quantize_mx(
+                out=w_codes[:, unit, :].bitcast(FP8X4),
+                scales=w_scales[:, unit, :],
+                in_=w_grouped[:, unit].rearrange("q c t -> q (c t)"),
+            )
+
+        tok = keep.tile([P, PAIRS, RUN, ROWS, PAIR * PACK], BF16, align_bytes=64)
+        tok_codes = keep.tile([P, PAIRS, RUN * P], U32, align_bytes=64)
+        tok_scales = keep.tile([P, PAIRS, RUN * P], U8, align_bytes=64)
+
+        def add_table(pair, chunk):
             chunk_rows = ROWS // TABLE_CHUNKS
-            for chunk in range(TABLE_CHUNKS):
-                span = slice(chunk * chunk_positions, (chunk + 1) * chunk_positions)
-                rows = slice(chunk * chunk_rows, (chunk + 1) * chunk_rows)
-                nc.vector.tensor_tensor(
-                    out=tok[:, pair, :, rows, :].rearrange("q r i g -> q i g r"),
-                    in0=x_rows[:, pair * PAIR * PACK : (pair + 1) * PAIR * PACK, span].rearrange(
-                        "q g (i r) -> q i g r", r=RUN
-                    ),
-                    in1=pe[:, :, span].rearrange("q g (i r) -> q i g r", r=RUN),
-                    op=ALU.add,
-                )
+            span = slice(chunk * chunk_positions, (chunk + 1) * chunk_positions)
+            rows = slice(chunk * chunk_rows, (chunk + 1) * chunk_rows)
+            nc.vector.tensor_tensor(
+                out=tok[:, pair, :, rows, :].rearrange("q r i g -> q i g r"),
+                in0=x_rows[:, pair * PAIR * PACK : (pair + 1) * PAIR * PACK, span].rearrange(
+                    "q g (i r) -> q i g r", r=RUN
+                ),
+                in1=pe[:, :, span].rearrange("q g (i r) -> q i g r", r=RUN),
+                op=ALU.add,
+            )
 
         def quantise_tokens(pair):
             for r in range(RUN):
@@ -206,40 +184,51 @@ def tile_multiheadselfattention_pa_kernel(tc, x, W_qkv, out_0, out_1, out_2):
                     in_=tok[:, pair, r].rearrange("q i g -> q (i g)"),
                 )
 
-        def project(pair, s, vector_helps):
-            stage = stage_pool.tile([P, HEADS, RUN, HEAD_DIM], F32)
-            for r in range(RUN):
-                acc = psum_acc.tile([P, PROJ_COLS], F32)
-                nc.tensor.matmul_mx(
-                    out=acc[:],
-                    lhsT=tok_codes[:, pair, r * P : (r + 1) * P].bitcast(FP8X4),
-                    lhsT_scale=tok_scales[:, pair, r * P : (r + 1) * P],
-                    rhs=w_codes[:, s, :].bitcast(FP8X4),
-                    rhs_scale=w_scales[:, s, :],
-                    start=True,
-                    stop=True,
-                )
-                by_head = acc[:].rearrange("m (h d) -> m h d", d=HEAD_DIM)
-                if vector_helps and r % 2 == 1:
-                    nc.vector.tensor_copy(out=stage[:, :, r, :], in_=by_head)
+        def project(pair, unit, vector_helps):
+            stage = stage_pool.tile([P, UNIT_HEADS, RUN, HEAD_DIM], F32)
+            for half in range(2):
+                acc = psum.tile([P, 2, UNIT_COLS], F32, tag="bank")
+                for k in range(2):
+                    r = 2 * half + k
+                    nc.tensor.matmul_mx(
+                        out=acc[:, k, :],
+                        lhsT=tok_codes[:, pair, r * P : (r + 1) * P].bitcast(FP8X4),
+                        lhsT_scale=tok_scales[:, pair, r * P : (r + 1) * P],
+                        rhs=w_codes[:, unit, :].bitcast(FP8X4),
+                        rhs_scale=w_scales[:, unit, :],
+                        start=True,
+                        stop=True,
+                    )
+                by_head = acc[:].rearrange("m k (h d) -> m h k d", d=HEAD_DIM)
+                if vector_helps and half == 1:
+                    nc.vector.tensor_copy(out=stage[:, :, 2 * half : 2 * half + 2, :], in_=by_head)
                 else:
-                    nc.scalar.copy(out=stage[:, :, r, :], in_=by_head)
+                    nc.scalar.copy(out=stage[:, :, 2 * half : 2 * half + 2, :], in_=by_head)
+            first_head = (unit % UNITS_PER_OUTPUT) * UNIT_HEADS
             for b in range(PAIR):
                 nc.sync.dma_start(
-                    out=outs[s][pair * PAIR + b].rearrange("h (i r) d -> i h (r d)", r=RUN),
+                    out=outs[unit // UNITS_PER_OUTPUT][
+                        pair * PAIR + b, first_head : first_head + UNIT_HEADS
+                    ].rearrange("h (i r) d -> i h (r d)", r=RUN),
                     in_=stage[b:P:PAIR].rearrange("m h r d -> m h (r d)"),
                 )
 
-        add_table(0)
+        flipped_w = [transpose_w(unit) for unit in range(UNITS)]
+        for unit in range(COPY_AHEAD):
+            group_w(unit)
+        for chunk in range(TABLE_CHUNKS):
+            add_table(0, chunk)
         quantise_w(0)
         quantise_tokens(0)
-        project(0, 0, True)
-        group_w(2, flipped_v)
         quantise_w(1)
-        quantise_w(2)
-        add_table(1)
+        for unit in range(UNITS):
+            project(0, unit, unit % 2 == 0)
+            if unit + COPY_AHEAD < UNITS:
+                group_w(unit + COPY_AHEAD)
+            if unit + QUANTISE_AHEAD < UNITS:
+                quantise_w(unit + QUANTISE_AHEAD)
+            if unit < TABLE_CHUNKS:
+                add_table(1, unit)
         quantise_tokens(1)
-        project(0, 1, False)
-        project(0, 2, False)
-        for s in range(PROJECTIONS):
-            project(1, s, True)
+        for unit in range(UNITS):
+            project(1, unit, True)

@@ -73,6 +73,12 @@ def tile_multiheadselfattention_pa_kernel(tc, x, W_qkv, out_0, out_1, out_2):
             )
         load_x(1)
 
+        zero_one = keep.tile([P, 2], F32)
+        nc.vector.memset(zero_one[:, 0:1], 0.0)
+        nc.vector.memset(zero_one[:, 1:2], 1.0)
+        warm = keep.tile([P, 1], F32)
+        nc.scalar.activation(out=warm[:], in_=zero_one[:, 0:1], func=ACT.Sin)
+
         chan_int = keep.tile([P, 2], I32)
         nc.gpsimd.iota(chan_int[:], pattern=[[1, 2]], base=0, channel_multiplier=2)
         base = keep.tile([P, 2], F32)
@@ -84,24 +90,26 @@ def tile_multiheadselfattention_pa_kernel(tc, x, W_qkv, out_0, out_1, out_2):
         ident = keep.tile([P, P], F32)
         make_identity(nc, ident[:])
 
-        warm = keep.tile([P, 2], F32)
-        nc.vector.memset(warm[:, 0:1], 0.0)
-        nc.scalar.activation(out=warm[:, 1:2], in_=warm[:, 0:1], func=ACT.Sin)
-        quarter_turn = keep.tile([P, 1], F32)
-        nc.vector.tensor_scalar_add(out=quarter_turn[:], in0=warm[:, 0:1], scalar1=0.5 * math.pi)
-
-        ones = keep.tile([P, POSITIONS], F32)
-        nc.vector.memset(ones[:], 1.0)
-        count = keep.tile([P, POSITIONS], F32)
-        nc.vector.tensor_tensor_scan(
-            out=count[:], data0=ones[:], data1=ones[:], initial=-1.0, op0=ALU.mult, op1=ALU.add
-        )
+        ones = zero_one[:, 1:2].to_broadcast([P, POSITIONS])
         pos = keep.tile([P, POSITIONS], F32)
-        nc.vector.tensor_scalar_mul(out=pos[:], in0=count[:], scalar1=1.0 / (2.0 * math.pi))
+        nc.vector.tensor_tensor_scan(
+            out=pos[:], data0=ones, data1=ones, initial=-1.0, op0=ALU.mult, op1=ALU.add
+        )
+        quarter_turn = keep.tile([P, 1], F32)
+        nc.vector.tensor_scalar_add(
+            out=quarter_turn[:], in0=zero_one[:, 0:1], scalar1=0.5 * math.pi
+        )
 
         turns = keep.tile([P, 2, POSITIONS], F32)
         for e in range(2):
-            nc.vector.tensor_scalar_mul(out=turns[:, e, :], in0=pos[:], scalar1=rate[:, e : e + 1])
+            nc.vector.tensor_scalar(
+                out=turns[:, e, :],
+                in0=pos[:],
+                scalar1=rate[:, e : e + 1],
+                scalar2=1.0 / (2.0 * math.pi),
+                op0=ALU.mult,
+                op1=ALU.mult,
+            )
         whole = keep.tile([P, 2, POSITIONS], F32)
         nc.vector.tensor_scalar(
             out=whole[:], in0=turns[:], scalar1=ROUND, scalar2=ROUND, op0=ALU.add, op1=ALU.subtract

@@ -2,7 +2,6 @@ import math
 from contextlib import ExitStack
 
 import concourse.mybir as mybir
-from concourse.masks import make_identity
 
 F32 = mybir.dt.float32
 BF16 = mybir.dt.bfloat16
@@ -73,12 +72,6 @@ def tile_multiheadselfattention_pa_kernel(tc, x, W_qkv, out_0, out_1, out_2):
             )
         load_x(1)
 
-        zero_one = keep.tile([P, 2], F32)
-        nc.vector.memset(zero_one[:, 0:1], 0.0)
-        nc.vector.memset(zero_one[:, 1:2], 1.0)
-        warm = keep.tile([P, 1], F32)
-        nc.scalar.activation(out=warm[:], in_=zero_one[:, 0:1], func=ACT.Sin)
-
         chan_int = keep.tile([P, 2], I32)
         nc.gpsimd.iota(chan_int[:], pattern=[[1, 2]], base=0, channel_multiplier=2)
         base = keep.tile([P, 2], F32)
@@ -87,29 +80,25 @@ def tile_multiheadselfattention_pa_kernel(tc, x, W_qkv, out_0, out_1, out_2):
         nc.vector.tensor_scalar_mul(out=exponent[:], in0=chan_int[:], scalar1=-1.0 / RATES)
         rate = keep.tile([P, 2], F32)
         nc.gpsimd.tensor_tensor(out=rate[:], in0=base[:], in1=exponent[:], op=ALU.pow)
-        ident = keep.tile([P, P], F32)
-        make_identity(nc, ident[:])
 
-        ones = zero_one[:, 1:2].to_broadcast([P, POSITIONS])
-        pos = keep.tile([P, POSITIONS], F32)
-        nc.vector.tensor_tensor_scan(
-            out=pos[:], data0=ones, data1=ones, initial=-1.0, op0=ALU.mult, op1=ALU.add
-        )
+        warm = keep.tile([P, 2], F32)
+        nc.vector.memset(warm[:, 0:1], 0.0)
+        nc.scalar.activation(out=warm[:, 1:2], in_=warm[:, 0:1], func=ACT.Sin)
         quarter_turn = keep.tile([P, 1], F32)
-        nc.vector.tensor_scalar_add(
-            out=quarter_turn[:], in0=zero_one[:, 0:1], scalar1=0.5 * math.pi
+        nc.vector.tensor_scalar_add(out=quarter_turn[:], in0=warm[:, 0:1], scalar1=0.5 * math.pi)
+
+        ones = keep.tile([P, POSITIONS], F32)
+        nc.vector.memset(ones[:], 1.0)
+        count = keep.tile([P, POSITIONS], F32)
+        nc.vector.tensor_tensor_scan(
+            out=count[:], data0=ones[:], data1=ones[:], initial=-1.0, op0=ALU.mult, op1=ALU.add
         )
+        pos = keep.tile([P, POSITIONS], F32)
+        nc.vector.tensor_scalar_mul(out=pos[:], in0=count[:], scalar1=1.0 / (2.0 * math.pi))
 
         turns = keep.tile([P, 2, POSITIONS], F32)
         for e in range(2):
-            nc.vector.tensor_scalar(
-                out=turns[:, e, :],
-                in0=pos[:],
-                scalar1=rate[:, e : e + 1],
-                scalar2=1.0 / (2.0 * math.pi),
-                op0=ALU.mult,
-                op1=ALU.mult,
-            )
+            nc.vector.tensor_scalar_mul(out=turns[:, e, :], in0=pos[:], scalar1=rate[:, e : e + 1])
         whole = keep.tile([P, 2, POSITIONS], F32)
         nc.vector.tensor_scalar(
             out=whole[:], in0=turns[:], scalar1=ROUND, scalar2=ROUND, op0=ALU.add, op1=ALU.subtract
@@ -119,6 +108,15 @@ def tile_multiheadselfattention_pa_kernel(tc, x, W_qkv, out_0, out_1, out_2):
         size = keep.tile([P, 2, POSITIONS], F32)
         nc.vector.scalar_tensor_tensor(
             out=size[:], in0=frac[:], scalar=-1.0, in1=frac[:], op0=ALU.mult, op1=ALU.max
+        )
+        ident = keep.tile([P, P], F32)
+        nc.vector.tensor_scalar(
+            out=ident[:],
+            in0=count[:, 0:P],
+            scalar1=-2.0 / RATES,
+            scalar2=exponent[:, 0:1],
+            op0=ALU.mult,
+            op1=ALU.is_equal,
         )
         pe = keep.tile([P, PAIR * PACK, POSITIONS], F32)
         pe_parts = pe[:].rearrange("q (b u e) n -> q b u e n", b=PAIR, u=2)

@@ -93,12 +93,17 @@ def tile_multiheadselfattention_pa_kernel(tc, x, W_qkv, out_0, out_1, out_2):
         nc.vector.tensor_tensor_scan(
             out=count[:], data0=ones[:], data1=ones[:], initial=-1.0, op0=ALU.mult, op1=ALU.add
         )
-        pos = keep.tile([P, POSITIONS], F32)
-        nc.vector.tensor_scalar_mul(out=pos[:], in0=count[:], scalar1=1.0 / (2.0 * math.pi))
 
         turns = keep.tile([P, 2, POSITIONS], F32)
         for e in range(2):
-            nc.vector.tensor_scalar_mul(out=turns[:, e, :], in0=pos[:], scalar1=rate[:, e : e + 1])
+            nc.vector.tensor_scalar(
+                out=turns[:, e, :],
+                in0=count[:],
+                scalar1=rate[:, e : e + 1],
+                scalar2=1.0 / (2.0 * math.pi),
+                op0=ALU.mult,
+                op1=ALU.mult,
+            )
         whole = keep.tile([P, 2, POSITIONS], F32)
         nc.vector.tensor_scalar(
             out=whole[:], in0=turns[:], scalar1=ROUND, scalar2=ROUND, op0=ALU.add, op1=ALU.subtract

@@ -72,6 +72,14 @@ def tile_multiheadselfattention_pa_kernel(tc, x, W_qkv, out_0, out_1, out_2):
             )
         load_x(1)
 
+        warm = keep.tile([P, 2], F32)
+        nc.vector.memset(warm[:, 0:1], 0.0)
+        nc.scalar.activation(out=warm[:, 1:2], in_=warm[:, 0:1], func=ACT.Sin)
+        quarter_turn = keep.tile([P, 1], F32)
+        nc.vector.tensor_scalar_add(out=quarter_turn[:], in0=warm[:, 0:1], scalar1=0.5 * math.pi)
+        ones = keep.tile([P, POSITIONS], F32)
+        nc.vector.memset(ones[:], 1.0)
+
         chan_int = keep.tile([P, 2], I32)
         nc.gpsimd.iota(chan_int[:], pattern=[[1, 2]], base=0, channel_multiplier=2)
         base = keep.tile([P, 2], F32)
@@ -81,14 +89,6 @@ def tile_multiheadselfattention_pa_kernel(tc, x, W_qkv, out_0, out_1, out_2):
         rate = keep.tile([P, 2], F32)
         nc.gpsimd.tensor_tensor(out=rate[:], in0=base[:], in1=exponent[:], op=ALU.pow)
 
-        warm = keep.tile([P, 2], F32)
-        nc.vector.memset(warm[:, 0:1], 0.0)
-        nc.scalar.activation(out=warm[:, 1:2], in_=warm[:, 0:1], func=ACT.Sin)
-        quarter_turn = keep.tile([P, 1], F32)
-        nc.vector.tensor_scalar_add(out=quarter_turn[:], in0=warm[:, 0:1], scalar1=0.5 * math.pi)
-
-        ones = keep.tile([P, POSITIONS], F32)
-        nc.vector.memset(ones[:], 1.0)
         count = keep.tile([P, POSITIONS], F32)
         nc.vector.tensor_tensor_scan(
             out=count[:], data0=ones[:], data1=ones[:], initial=-1.0, op0=ALU.mult, op1=ALU.add

@@ -72,14 +72,6 @@ def tile_multiheadselfattention_pa_kernel(tc, x, W_qkv, out_0, out_1, out_2):
             )
         load_x(1)
 
-        warm = keep.tile([P, 2], F32)
-        nc.vector.memset(warm[:, 0:1], 0.0)
-        nc.scalar.activation(out=warm[:, 1:2], in_=warm[:, 0:1], func=ACT.Sin)
-        quarter_turn = keep.tile([P, 1], F32)
-        nc.vector.tensor_scalar_add(out=quarter_turn[:], in0=warm[:, 0:1], scalar1=0.5 * math.pi)
-        ones = keep.tile([P, POSITIONS], F32)
-        nc.vector.memset(ones[:], 1.0)
-
         chan_int = keep.tile([P, 2], I32)
         nc.gpsimd.iota(chan_int[:], pattern=[[1, 2]], base=0, channel_multiplier=2)
         base = keep.tile([P, 2], F32)
@@ -89,9 +81,18 @@ def tile_multiheadselfattention_pa_kernel(tc, x, W_qkv, out_0, out_1, out_2):
         rate = keep.tile([P, 2], F32)
         nc.gpsimd.tensor_tensor(out=rate[:], in0=base[:], in1=exponent[:], op=ALU.pow)
 
+        warm = keep.tile([P, 2], F32)
+        nc.vector.memset(warm[:, 0:1], 0.0)
+        nc.scalar.activation(out=warm[:, 1:2], in_=warm[:, 0:1], func=ACT.Sin)
+        quarter_turn = keep.tile([P, 1], F32)
+        nc.vector.tensor_scalar_add(out=quarter_turn[:], in0=warm[:, 0:1], scalar1=0.5 * math.pi)
+
+        one = keep.tile([P, 1], F32)
+        nc.vector.memset(one[:], 1.0)
+        ones = one[:].to_broadcast([P, POSITIONS])
         count = keep.tile([P, POSITIONS], F32)
         nc.vector.tensor_tensor_scan(
-            out=count[:], data0=ones[:], data1=ones[:], initial=-1.0, op0=ALU.mult, op1=ALU.add
+            out=count[:], data0=ones, data1=ones, initial=-1.0, op0=ALU.mult, op1=ALU.add
         )
 
         turns = keep.tile([P, 2, POSITIONS], F32)

import math
from contextlib import ExitStack

import concourse.mybir as mybir

F32 = mybir.dt.float32
BF16 = mybir.dt.bfloat16
I32 = mybir.dt.int32
U32 = mybir.dt.uint32
U8 = mybir.dt.uint8
FP8X4 = mybir.dt.float8_e4m3fn_x4
ALU = mybir.AluOpType
ACT = mybir.ActivationFunctionType

P = 128
PACK = 4
IMAGES = 4
CHANNELS = 512
POSITIONS = 256
HEAD_DIM = 64
BANK = 512

PAIR = 2
PAIRS = IMAGES // PAIR
RUN = 4
ROWS = POSITIONS // RUN
TABLE_CHUNKS = 4

UNIT_HEADS = 4
UNIT_COLS = UNIT_HEADS * HEAD_DIM
UNIT_BLOCKS = UNIT_COLS // P
UNITS = 6
UNITS_PER_OUTPUT = 2
COPY_AHEAD = 4
QUANTISE_AHEAD = 2

RATES = CHANNELS // 2
ROUND = 1.5 * 2.0**23

FLOPS = 2 * IMAGES * POSITIONS * CHANNELS * UNITS * UNIT_COLS


def tile_multiheadselfattention_pa_kernel(tc, x, W_qkv, out_0, out_1, out_2):
    nc = tc.nc
    outs = (out_0, out_1, out_2)
    with ExitStack() as pools:
        keep = pools.enter_context(tc.tile_pool(name="keep", bufs=1))
        stage_pool = pools.enter_context(tc.tile_pool(name="stage", bufs=6))
        psum = pools.enter_context(tc.psum_pool(name="psum", bufs=8))
        pools.enter_context(tc.manual_schedule())

        x_rows = keep.tile([P, IMAGES * PACK, POSITIONS], BF16)
        w_rows = keep.tile([P, UNITS, UNIT_BLOCKS, CHANNELS], BF16)

        def load_x(pair):
            nc.sync.dma_start(
                out=x_rows[:, pair * PAIR * PACK : (pair + 1) * PAIR * PACK, :].rearrange(
                    "q (b u e) n -> q b u (e n)", b=PAIR, u=2
                ),
                in_=x[pair * PAIR : (pair + 1) * PAIR].rearrange(
                    "b (u q e) h w -> q b u (e h w)", u=2, e=2
                ),
            )

        load_x(0)
        for unit in range(UNITS):
            nc.sync.dma_start(
                out=w_rows[:, unit],
                in_=W_qkv[unit * UNIT_COLS : (unit + 1) * UNIT_COLS, :].rearrange(
                    "(g o) c -> o g c", o=P
                ),
            )
        load_x(1)

        chan_int = keep.tile([P, 2], I32)
        nc.gpsimd.iota(chan_int[:], pattern=[[1, 2]], base=0, channel_multiplier=2)
        base = keep.tile([P, 2], F32)
        nc.gpsimd.memset(base[:], 10000.0)
        exponent = keep.tile([P, 2], F32)
        nc.vector.tensor_scalar_mul(out=exponent[:], in0=chan_int[:], scalar1=-1.0 / RATES)
        rate = keep.tile([P, 2], F32)
        nc.gpsimd.tensor_tensor(out=rate[:], in0=base[:], in1=exponent[:], op=ALU.pow)

        warm = keep.tile([P, 2], F32)
        nc.vector.memset(warm[:, 0:1], 0.0)
        nc.scalar.activation(out=warm[:, 1:2], in_=warm[:, 0:1], func=ACT.Sin)
        quarter_turn = keep.tile([P, 1], F32)
        nc.vector.tensor_scalar_add(out=quarter_turn[:], in0=warm[:, 0:1], scalar1=0.5 * math.pi)

        one = keep.tile([P, 1], F32)
        nc.vector.memset(one[:], 1.0)
        ones = one[:].to_broadcast([P, POSITIONS])
        count = keep.tile([P, POSITIONS], F32)
        nc.vector.tensor_tensor_scan(
            out=count[:], data0=ones, data1=ones, initial=-1.0, op0=ALU.mult, op1=ALU.add
        )

        turns = keep.tile([P, 2, POSITIONS], F32)
        for e in range(2):
            nc.vector.tensor_scalar(
                out=turns[:, e, :],
                in0=count[:],
                scalar1=rate[:, e : e + 1],
                scalar2=1.0 / (2.0 * math.pi),
                op0=ALU.mult,
                op1=ALU.mult,
            )
        whole = keep.tile([P, 2, POSITIONS], F32)
        nc.vector.tensor_scalar(
            out=whole[:], in0=turns[:], scalar1=ROUND, scalar2=ROUND, op0=ALU.add, op1=ALU.subtract
        )
        frac = keep.tile([P, 2, POSITIONS], F32)
        nc.vector.tensor_tensor(out=frac[:], in0=turns[:], in1=whole[:], op=ALU.subtract)
        size = keep.tile([P, 2, POSITIONS], F32)
        nc.vector.scalar_tensor_tensor(
            out=size[:], in0=frac[:], scalar=-1.0, in1=frac[:], op0=ALU.mult, op1=ALU.max
        )
        ident = keep.tile([P, P], F32)
        nc.vector.tensor_scalar(
            out=ident[:],
            in0=count[:, 0:P],
            scalar1=-2.0 / RATES,
            scalar2=exponent[:, 0:1],
            op0=ALU.mult,
            op1=ALU.is_equal,
        )
        pe = keep.tile([P, PAIR * PACK, POSITIONS], F32)
        pe_parts = pe[:].rearrange("q (b u e) n -> q b u e n", b=PAIR, u=2)
        chunk_positions = POSITIONS // TABLE_CHUNKS
        for chunk in range(TABLE_CHUNKS):
            span = slice(chunk * chunk_positions, (chunk + 1) * chunk_positions)
            both = [P, PAIR, 2, chunk_positions]
            nc.scalar.activation(
                out=pe_parts[:, :, 0, :, span],
                in_=frac[:, :, span].unsqueeze(1).to_broadcast(both),
                func=ACT.Sin,
                scale=2.0 * math.pi,
            )
            nc.scalar.activation(
                out=pe_parts[:, :, 1, :, span],
                in_=size[:, :, span].unsqueeze(1).to_broadcast(both),
                func=ACT.Sin,
                scale=-2.0 * math.pi,
                bias=quarter_turn[:],
            )

        w_grouped = keep.tile([P, UNITS, UNIT_COLS, PACK], BF16, align_bytes=64)
        w_codes = keep.tile([P, UNITS, UNIT_COLS], U32, align_bytes=64)
        w_scales = keep.tile([P, UNITS, UNIT_COLS], U8, align_bytes=64)

        def transpose_w(unit):
            words = w_rows[:, unit].bitcast(F32)
            flipped = psum.tile([P, UNIT_BLOCKS, 2, P], F32, tag="bank")
            for g in range(UNIT_BLOCKS):
                for u in range(2):
                    nc.tensor.transpose(
                        flipped[:, g, u, :], words[:, g, u * P : (u + 1) * P], ident[:]
                    )
            return flipped

        def group_w(unit):
            nc.scalar.copy(
                out=w_grouped[:, unit].bitcast(F32).rearrange("q (g o) u -> q g o u", g=UNIT_BLOCKS),
                in_=flipped_w[unit][:].rearrange("q g u o -> q g o u"),
            )

        def quantise_w(unit):
            nc.vector.quantize_mx(
                out=w_codes[:, unit, :].bitcast(FP8X4),
                scales=w_scales[:, unit, :],
                in_=w_grouped[:, unit].rearrange("q c t -> q (c t)"),
            )

        tok = keep.tile([P, PAIRS, RUN, ROWS, PAIR * PACK], BF16, align_bytes=64)
        tok_codes = keep.tile([P, PAIRS, RUN * P], U32, align_bytes=64)
        tok_scales = keep.tile([P, PAIRS, RUN * P], U8, align_bytes=64)

        def add_table(pair, chunk):
            chunk_rows = ROWS // TABLE_CHUNKS
            span = slice(chunk * chunk_positions, (chunk + 1) * chunk_positions)
            rows = slice(chunk * chunk_rows, (chunk + 1) * chunk_rows)
            nc.vector.tensor_tensor(
                out=tok[:, pair, :, rows, :].rearrange("q r i g -> q i g r"),
                in0=x_rows[:, pair * PAIR * PACK : (pair + 1) * PAIR * PACK, span].rearrange(
                    "q g (i r) -> q i g r", r=RUN
                ),
                in1=pe[:, :, span].rearrange("q g (i r) -> q i g r", r=RUN),
                op=ALU.add,
            )

        def quantise_tokens(pair):
            for r in range(RUN):
                nc.vector.quantize_mx(
                    out=tok_codes[:, pair, r * P : (r + 1) * P].bitcast(FP8X4),
                    scales=tok_scales[:, pair, r * P : (r + 1) * P],
                    in_=tok[:, pair, r].rearrange("q i g -> q (i g)"),
                )

        def project(pair, unit, vector_helps):
            stage = stage_pool.tile([P, UNIT_HEADS, RUN, HEAD_DIM], F32)
            for half in range(2):
                acc = psum.tile([P, 2, UNIT_COLS], F32, tag="bank")
                for k in range(2):
                    r = 2 * half + k
                    nc.tensor.matmul_mx(
                        out=acc[:, k, :],
                        lhsT=tok_codes[:, pair, r * P : (r + 1) * P].bitcast(FP8X4),
                        lhsT_scale=tok_scales[:, pair, r * P : (r + 1) * P],
                        rhs=w_codes[:, unit, :].bitcast(FP8X4),
                        rhs_scale=w_scales[:, unit, :],
                        start=True,
                        stop=True,
                    )
                by_head = acc[:].rearrange("m k (h d) -> m h k d", d=HEAD_DIM)
                if vector_helps and half == 1:
                    nc.vector.tensor_copy(out=stage[:, :, 2 * half : 2 * half + 2, :], in_=by_head)
                else:
                    nc.scalar.copy(out=stage[:, :, 2 * half : 2 * half + 2, :], in_=by_head)
            first_head = (unit % UNITS_PER_OUTPUT) * UNIT_HEADS
            for b in range(PAIR):
                nc.sync.dma_start(
                    out=outs[unit // UNITS_PER_OUTPUT][
                        pair * PAIR + b, first_head : first_head + UNIT_HEADS
                    ].rearrange("h (i r) d -> i h (r d)", r=RUN),
                    in_=stage[b:P:PAIR].rearrange("m h r d -> m h (r d)"),
                )

        flipped_w = [transpose_w(unit) for unit in range(UNITS)]
        for unit in range(COPY_AHEAD):
            group_w(unit)
        for chunk in range(TABLE_CHUNKS):
            add_table(0, chunk)
        quantise_w(0)
        quantise_tokens(0)
        quantise_w(1)
        for unit in range(UNITS):
            project(0, unit, unit % 2 == 0)
            if unit + COPY_AHEAD < UNITS:
                group_w(unit + COPY_AHEAD)
            if unit + QUANTISE_AHEAD < UNITS:
                quantise_w(unit + QUANTISE_AHEAD)
            if unit < TABLE_CHUNKS:
                add_table(1, unit)
        quantise_tokens(1)
        for unit in range(UNITS):
            project(1, unit, True)
